import numpy as np
import ml_dtypes


def mxq(x, axis, fmt="e4m3"):
    dtype, down = {"e4m3": (ml_dtypes.float8_e4m3fn, 7), "e5m2": (ml_dtypes.float8_e5m2, 14)}[fmt]
    v = np.moveaxis(np.asarray(x, np.float32).astype(ml_dtypes.bfloat16).astype(np.float64), axis, -1)
    blocks = v.reshape(v.shape[:-1] + (-1, 32))
    amax = np.abs(blocks).max(-1, keepdims=True)
    byte = np.maximum(np.where(amax > 0, np.frexp(amax)[1] - 1 + 127, 0) - down, 1)
    scale = np.exp2(byte - 127.0)
    codes = (blocks / scale).astype(np.float32).astype(dtype).astype(np.float64)
    return np.moveaxis((codes * scale).reshape(v.shape), -1, axis)


WIDE = False


def mx_kscale(k):
    if not WIDE:
        return np.ones(k)
    levels = np.array([18, -18])
    if k % 512:
        return np.exp2(np.random.permutation(np.resize(levels, k // 32))).repeat(32)
    a = np.empty((k // 512, 16))
    for p in range(k // 512):
        a[p, :8] = np.random.permutation(np.resize(levels, 8))
        for g in range(8):
            far = levels[np.abs(levels - a[p, g]) >= 10]
            a[p, g + 8] = far[np.random.randint(len(far))]
    return np.exp2(a.ravel()).repeat(32)


BF16 = ml_dtypes.bfloat16


def bf(x):
    return np.asarray(x, np.float32).astype(BF16)


def f64(x):
    return np.asarray(x).astype(np.float64)


B, H, A = 512, 1024, 1024


def setup_inputs():
    s = mx_kscale(B)[:, None]
    u = mx_kscale(A)
    x0 = bf(np.random.standard_normal((B, H)))
    alpha0 = bf(np.random.standard_normal((B, H)))
    aa = bf(np.random.standard_normal((B, A)) * 0.5)
    bb = bf(np.random.uniform(0.5, 1.5, (B, A)))
    pp = bf(np.random.standard_normal((B, A)))
    time_decay = bf(-1.0 + 1.5 * np.random.standard_normal(A))
    time_first = bf(-1.2 + 0.5 * np.random.standard_normal(A))
    time_mix_k = bf(np.random.uniform(0.1, 0.9, H))
    time_mix_v = bf(np.random.uniform(0.2, 1.1, H))
    Wk0 = bf(np.random.standard_normal((A, H)) * 1.5 / np.sqrt(H))
    Wv0 = bf(np.random.standard_normal((A, H)) * 1.2 / np.sqrt(H))
    grads = [
        bf(2.0 * np.random.standard_normal((B, A)) * np.exp2(np.random.randint(-6, 1, (B, 1))) / s * u)
        for _ in range(4)
    ]
    tk, tv = f64(time_mix_k), f64(time_mix_v)
    k = (f64(x0) * tk + f64(alpha0) * (1.0 - tk)) @ f64(Wk0).T
    v = (f64(x0) * tv + f64(alpha0) * (1.0 - tv)) @ f64(Wv0).T
    gap = f64(pp) + f64(time_decay) - k
    pp = bf(np.where(np.abs(gap) < 0.03125, f64(pp) + np.where(gap >= 0.0, 0.25, -0.25), f64(pp)))
    return {
        "x": bf(f64(x0) * s),
        "alpha": bf(f64(alpha0) * s),
        "aa": aa,
        "bb": bb,
        "pp": pp,
        "time_decay": time_decay,
        "time_first": time_first,
        "time_mix_k": time_mix_k,
        "time_mix_v": time_mix_v,
        "Wk": bf(f64(Wk0) / u[:, None]),
        "Wv": bf(f64(Wv0) / u[:, None]),
        "k": np.asarray(k, np.float32),
        "v": np.asarray(v, np.float32),
        "grad_0": grads[0],
        "grad_1": grads[1],
        "grad_2": grads[2],
        "grad_3": grads[3],
    }


def reference(x, alpha, aa, bb, pp, time_decay, time_first, time_mix_k, time_mix_v, Wk, Wv, k, v, grad_0, grad_1, grad_2, grad_3):
    x, alpha, aa, bb, pp = f64(x), f64(alpha), f64(aa), f64(bb), f64(pp)
    time_decay, time_first = f64(time_decay), f64(time_first)
    time_mix_k, time_mix_v = f64(time_mix_k), f64(time_mix_v)
    Wk, Wv, k, v = f64(Wk), f64(Wv), f64(k), f64(v)
    g0, g1, g2, g3 = f64(grad_0), f64(grad_1), f64(grad_2), f64(grad_3)
    ww = time_first + k
    qq = np.maximum(pp, ww)
    e1 = np.exp(pp - qq)
    e2 = np.exp(ww - qq)
    den = e1 * bb + e2
    ww2 = pp + time_decay
    qq2 = np.maximum(ww2, k)
    e1b = np.exp(ww2 - qq2)
    e2b = np.exp(k - qq2)
    dv = g0 * e2 / den + g1 * e2b
    dk_out = g0 * e1 * e2 * (bb * v - aa) / (den * den)
    dk_state = np.where(k > ww2, g3 - e1b * (g1 * aa + g2 * bb), e2b * (g1 * v + g2))
    dk = dk_out + dk_state
    dz = np.concatenate([dk, dv], axis=1)
    wj = np.concatenate([Wk * time_mix_k, Wv * time_mix_v], axis=0)
    dx = mxq(dz, 1, "e5m2") @ mxq(wj, 0, "e4m3")
    xk = x * time_mix_k + alpha * (1.0 - time_mix_k)
    xv = x * time_mix_v + alpha * (1.0 - time_mix_v)
    dWk = mxq(dk, 0, "e5m2").T @ mxq(xk, 0, "e4m3")
    dWv = mxq(dv, 0, "e5m2").T @ mxq(xv, 0, "e4m3")
    return dx, dWk, dWv

from contextlib import ExitStack
import math

import concourse.mybir as mybir
from concourse.masks import make_identity

B, H, A = 512, 1024, 1024
FLOPS = 2 * B * 2 * A * H + 2 * 2 * A * B * H

F32 = mybir.dt.float32
BF16 = mybir.dt.bfloat16
U32 = mybir.dt.uint32
U8 = mybir.dt.uint8
E4 = mybir.dt.float8_e4m3fn_x4
E5 = mybir.dt.float8_e5m2_x4
ACT = mybir.ActivationFunctionType
ALU = mybir.AluOpType

P = 128
J = 4
CH = 128
N_CH = A // CH
HALF = 512
LN2 = math.log(2.0)


def tile_rwkvtimemix_pa_v_kernel(
    tc, x, alpha, aa, bb, pp, time_decay, time_first, time_mix_k, time_mix_v, Wk, Wv, k, v,
    grad_0, grad_1, grad_2, grad_3, out_0, out_1, out_2,
):
    nc = tc.nc
    with ExitStack() as ctx:
        const = ctx.enter_context(tc.tile_pool(name="const", bufs=1))
        sb = ctx.enter_context(tc.tile_pool(name="sb", bufs=2))
        ps = ctx.enter_context(tc.psum_pool(name="ps", bufs=1))

        def psum(name, tag, bufs, shape, dt):
            t = ps.tile(shape, dt, name=name, tag=tag, bufs=bufs)
            return t

        def ps_tc(shape, dt):
            return psum("tcb", "tcb", 3, shape, dt)

        def ps_mm(shape, dt):
            return psum("mmb", "mmb", 2, shape, dt)

        def ps_nd():
            return psum("ndb", "ndb", 2, [P, J, P], F32)

        def ps_sum():
            return psum("sumb", "sumb", 1, [P, J, CH], F32)

        ident = const.tile([P, P], F32, name="ident")
        make_identity(nc, ident[:])
        identb = const.tile([P, P], BF16, name="identb")
        make_identity(nc, identb[:])

        def tr32(out, in_, start=True, stop=True):
            nc.tensor.matmul(out, lhsT=in_, rhs=ident[:], start=start, stop=stop, is_transpose=True)

        def tr16(out, in_):
            nc.tensor.transpose(out, in_, identb[:])

        def half_view(t, h):
            return t.rearrange("(p j) c -> p j c", j=J)[:, :, h * HALF:(h + 1) * HALF]

        def load16(t, h):
            r = sb.tile([P, J, HALF], BF16, name="in16", tag="in16", bufs=16)
            nc.sync.dma_start(out=r[:], in_=half_view(t, h))
            return r

        def load32(t, h):
            r = sb.tile([P, J, HALF], F32, name="in32", tag="in32", bufs=4, align_bytes=64)
            nc.sync.dma_start(out=r[:], in_=half_view(t, h))
            return r

        vrow = const.tile([P, P], BF16, name="vrow")
        nc.vector.memset(vrow[:], 0.0)
        inp = {}
        inp["pp", 0] = load16(pp, 0)
        inp["k", 0] = load32(k, 0)
        for i, vec in enumerate((time_decay, time_first, time_mix_k, time_mix_v)):
            nc.sync.dma_start(out=vrow[8 * i:8 * i + 8, :], in_=vec.rearrange("(b p) -> b p", p=P))
        inp["bb", 0] = load16(bb, 0)
        inp["bb", 1] = load16(bb, 1)
        inp["g1", 0] = load16(grad_1, 0)
        inp["aa", 0] = load16(aa, 0)
        xh = [load16(x, 0)]
        ah = [load16(alpha, 0)]
        inp["v", 0] = load32(v, 0)
        inp["g2", 0] = load16(grad_2, 0)
        inp["g0", 0] = load16(grad_0, 0)
        inp["g3", 0] = load16(grad_3, 0)
        xh.append(load16(x, 1))
        ah.append(load16(alpha, 1))
        for nm, t in (("pp", pp), ("k", k), ("g1", grad_1), ("aa", aa), ("v", v), ("g2", grad_2), ("g0", grad_0), ("g3", grad_3)):
            inp[nm, 1] = load32(t, 1) if nm in ("k", "v") else load16(t, 1)
        tm_b = []
        for vec in (time_mix_k, time_mix_v):
            t = const.tile([P, H], BF16, name="tmb%d" % len(tm_b))
            nc.sync.dma_start(out=t[:], in_=vec.partition_broadcast(P))
            tm_b.append(t)

        vps = ps_mm([P, P], BF16)
        tr16(vps[:], vrow[:])
        cols = const.tile([P, 32], F32, name="cols")
        nc.vector.tensor_copy(out=cols[:], in_=vps[:, 0:32])
        td = cols[:, 0:8]
        htf = const.tile([P, 8], F32, name="htf")
        nc.vector.tensor_scalar(out=htf[:], in0=cols[:, 8:16], scalar1=0.5, scalar2=None, op0=ALU.mult)
        ntd = const.tile([P, 8], F32, name="ntd")
        nc.vector.tensor_scalar(out=ntd[:], in0=td, scalar1=-1.0, scalar2=None, op0=ALU.mult)
        ntdl = const.tile([P, 8], F32, name="ntdl")
        nc.vector.tensor_scalar(out=ntdl[:], in0=td, scalar1=-1.0, scalar2=LN2, op0=ALU.mult, op1=ALU.add)
        omt = const.tile([P, 16], F32, name="omt")
        nc.vector.tensor_scalar(out=omt[:], in0=cols[:, 16:32], scalar1=-1.0, scalar2=1.0, op0=ALU.mult, op1=ALU.add)

        logb = []
        for h in range(2):
            t = const.tile([P, J, HALF], F32, name="logb%d" % h)
            nc.scalar.activation(out=t[:], in_=inp["bb", h][:], func=ACT.Ln)
            logb.append(t)

        def stage_t(b):
            h, c = divmod(b * CH, HALF)
            s = slice(c, c + CH)

            def prod():
                return sb.tile([P, J, CH], F32, name="pr", tag="pr", bufs=8)

            def src(nm):
                return inp[nm, h][:, :, s]

            if b % 4 == 0:
                nc.vector.tensor_scalar(out=inp["aa", h][:], in0=inp["aa", h][:], scalar1=-1.0, scalar2=None, op0=ALU.mult)
            ib = sb.tile([P, J, CH], F32, name="ib", tag="ib", bufs=2)
            nc.scalar.activation(out=ib[:], in_=logb[h][:, :, s], func=ACT.Exp, scale=-1.0)
            r = {}
            for nm in ("nc", "nab", "gv", "g2", "ga", "gb"):
                r[nm] = prod()
            nc.gpsimd.tensor_tensor(out=r["nc"][:], in0=src("pp"), in1=src("k"), op=ALU.subtract)
            nc.gpsimd.tensor_tensor(out=r["nab"][:], in0=src("aa"), in1=ib[:], op=ALU.mult)
            nc.gpsimd.tensor_tensor(out=r["gv"][:], in0=src("g1"), in1=src("v"), op=ALU.mult)
            nc.gpsimd.tensor_scalar(out=r["g2"][:], in0=src("g2"), scalar1=1.0, scalar2=0.0, op0=ALU.mult, op1=ALU.add)
            nc.gpsimd.tensor_tensor(out=r["ga"][:], in0=src("g1"), in1=src("aa"), op=ALU.mult)
            nc.gpsimd.tensor_tensor(out=r["gb"][:], in0=src("g2"), in1=src("bb"), op=ALU.mult)
            return r

        def ctile(tag):
            return sb.tile([P, J, P], F32, name="ct" + tag, tag="ct" + tag, bufs=2)

        def stage_c(b, r):
            h, c = divmod(b * CH, HALF)
            s = slice(c, c + CH)
            col = slice(b, b + 1)
            nd = ps_nd()
            for j in range(J):
                tr32(nd[:, j, :], r["nc"][:, j, :])
            nz = ps_tc([P, J, P], F32)
            for j in range(J):
                tr32(nz[:, j, :], r["nc"][:, j, :], True, False)
                tr32(nz[:, j, :], logb[h][:, j, s], False, True)
            e = ctile("e")
            nc.scalar.activation(out=e[:], in_=nd[:], func=ACT.Abs, bias=td[:, col])
            nc.scalar.activation(out=e[:], in_=e[:], func=ACT.Exp, scale=-1.0)
            g1x = ctile("g1x")
            nc.scalar.activation(out=g1x[:], in_=nd[:], func=ACT.Exp, scale=-1.0, bias=ntdl[:, col])
            th = ctile("th")
            nc.scalar.activation(out=th[:], in_=nz[:], func=ACT.Tanh, scale=-0.5, bias=htf[:, col])
            gg = ps_tc([P, 2, J, P], BF16)
            for j in range(J):
                tr16(gg[:, 0, j, :], inp["g0", h][:, j, s])
                tr16(gg[:, 1, j, :], inp["g1", h][:, j, s])
            q2 = ctile("q2")
            nc.vector.scalar_tensor_tensor(out=q2[:], in0=g1x[:], scalar=2.0, in1=gg[:, 1], op0=ALU.min, op1=ALU.mult)
            p2 = ctile("p2")
            nc.vector.scalar_tensor_tensor(out=p2[:], in0=th[:], scalar=1.0, in1=gg[:, 0], op0=ALU.add, op1=ALU.mult)
            am = ps_tc([P, J, P], F32)
            for j in range(J):
                tr32(am[:, j, :], r["ga"][:, j, :], True, False)
                tr32(am[:, j, :], r["gb"][:, j, :], False, True)
            ta = ctile("ta")
            nc.vector.tensor_tensor(out=ta[:], in0=am[:], in1=e[:], op=ALU.mult)
            g3 = ps_tc([P, J, P], BF16)
            for j in range(J):
                tr16(g3[:, j, :], inp["g3", h][:, j, s])
            f2 = ctile("f2")
            nc.vector.scalar_tensor_tensor(out=f2[:], in0=nd[:], scalar=ntd[:, col], in1=e[:], op0=ALU.is_ge, op1=ALU.mult)
            nc.vector.tensor_tensor(out=ta[:], in0=g3[:], in1=ta[:], op=ALU.add)
            u = ps_tc([P, J, P], F32)
            for j in range(J):
                tr32(u[:, j, :], inp["v", h][:, j, s], True, False)
                tr32(u[:, j, :], r["nab"][:, j, :], False, True)
            nc.vector.scalar_tensor_tensor(out=th[:], in0=th[:], scalar=1.0, in1=u[:], op0=ALU.subtract, op1=ALU.mult)
            nc.vector.scalar_tensor_tensor(out=ta[:], in0=nd[:], scalar=ntd[:, col], in1=ta[:], op0=ALU.is_lt, op1=ALU.mult)
            y = ps_tc([P, J, P], F32)
            for j in range(J):
                tr32(y[:, j, :], r["gv"][:, j, :], True, False)
                tr32(y[:, j, :], r["g2"][:, j, :], False, True)
            nc.vector.tensor_tensor(out=f2[:], in0=y[:], in1=f2[:], op=ALU.mult)
            nc.vector.scalar_tensor_tensor(out=th[:], in0=p2[:], scalar=-0.25, in1=th[:], op0=ALU.mult, op1=ALU.mult)
            return {"dv": (p2, q2), "dk": (ta, f2, th)}

        t2 = {}
        dq = {}

        def stage_s(b, parts):
            g, bi = divmod(b, 4)
            codes = sb.tile([P, 2, CH], U32, name="dqc", tag="dqc", bufs=3, align_bytes=64)
            scales = sb.tile([P, 2, CH], U8, name="dqs", tag="dqs", bufs=3, align_bytes=64)
            for i, (nm, sc) in enumerate((("dk", 1.0), ("dv", 0.5))):
                if bi == 0:
                    t2[nm, g] = sb.tile([P, HALF, J], BF16, name="t2" + nm, tag="t2" + nm, bufs=1, align_bytes=64)
                acc = ps_sum()
                for j in range(J):
                    for n, t in enumerate(parts[nm]):
                        tr32(acc[:, j, :], t[:, j, :], n == 0, n == len(parts[nm]) - 1)
                dst = t2[nm, g][:, bi * CH:(bi + 1) * CH, :]
                nc.scalar.activation(out=dst, in_=acc[:].rearrange("p j c -> p c j"), func=ACT.Copy, scale=sc)
                nc.vector.quantize_mx(
                    out=codes[:, i, :].bitcast(E5),
                    scales=scales[:, i, :],
                    in_=dst.rearrange("p c j -> p (c j)"),
                )
            return codes, scales

        def stage_w(b, codes, scales):
            for i, out in enumerate((out_1, out_2)):
                ot = sb.tile([P, H], F32, name="ot", tag="ot", bufs=3)
                for n in range(2):
                    acc = ps_mm([P, HALF], F32)
                    ns = slice(n * HALF, (n + 1) * HALF)
                    nc.tensor.matmul_mx(
                        out=acc[:], lhsT=codes[:, i, :].bitcast(E5), lhsT_scale=scales[:, i, :],
                        rhs=xq[i][:, ns].bitcast(E4), rhs_scale=xs[i][:, ns], start=True, stop=True,
                    )
                    nc.scalar.copy(out=ot[:, ns], in_=acc[:])
                nc.sync.dma_start(out=out[b * CH:(b + 1) * CH, :], in_=ot[:])

        cq = {}

        def stage_b(g):
            for nm in ("dv", "dk"):
                words = t2[nm, g][:].rearrange("p c j -> p (c j)").bitcast(F32)
                ct = sb.tile([P, J, P, 4], BF16, name="cb", tag="cb", bufs=2, align_bytes=64)
                for jp in range(2):
                    bank = ps_tc([P, 4, P], F32)
                    for t in range(4):
                        tr32(bank[:, t, :], words[:, 2 * t + jp:2 * t + jp + 8 * (P - 1) + 1:8])
                    src = bank[:].rearrange("q t p -> q (t p)").bitcast(BF16).rearrange("q (t p e) -> q e p t", t=4, e=2)
                    nc.scalar.copy(out=ct[:, 2 * jp:2 * jp + 2, :, :], in_=src)
                codes = const.tile([P, B], U32, name="cq%s%d" % (nm, g), align_bytes=64)
                scales = const.tile([P, B], U8, name="cs%s%d" % (nm, g), align_bytes=64)
                nc.vector.quantize_mx(out=codes[:].bitcast(E5), scales=scales[:], in_=ct[:].rearrange("q j p t -> q (j p t)"))
                cq[nm, g] = (codes, scales)

        xq, xs = [], []
        for i in range(2):
            t = const.tile([P, H], U32, name="xq%d" % i, align_bytes=64)
            xq.append(t)
            t = const.tile([P, H], U8, name="xs%d" % i, align_bytes=64)
            xs.append(t)

        def il_tile():
            return sb.tile([P, HALF, 4], BF16, name="il", tag="il", bufs=3, align_bytes=64)

        def x_half(h):
            il = [il_tile(), il_tile()]
            for bi in range(4):
                s = slice(bi * CH, (bi + 1) * CH)
                hb = 4 * h + bi
                raw = ps_tc([P, 2, J, P], BF16)
                for j in range(J):
                    tr16(raw[:, 0, j, :], xh[h][:, j, s])
                    tr16(raw[:, 1, j, :], ah[h][:, j, s])
                w = ps_mm([P, 2, 2, P], F32)
                for i in range(2):
                    tmx = ctile(("ta", "f2")[i])
                    nc.scalar.activation(out=tmx[:], in_=raw[:, 0], func=ACT.Copy, scale=cols[:, 16 + 8 * i + hb:17 + 8 * i + hb])
                    xc = sb.tile([P, P, J], BF16, name="xc", tag="xc", bufs=3)
                    nc.vector.scalar_tensor_tensor(
                        out=xc[:], in0=raw[:, 1].rearrange("c j p -> c p j"), scalar=omt[:, 8 * i + hb:8 * i + hb + 1],
                        in1=tmx[:].rearrange("c j p -> c p j"), op0=ALU.mult, op1=ALU.add,
                    )
                    xw = xc[:].rearrange("c p j -> c (p j)").bitcast(F32)
                    for uu in range(2):
                        tr32(w[:, i, uu, :], xw[:, uu:uu + 2 * (P - 1) + 1:2])
                for i in range(2):
                    dst = il[i][:, s, :].rearrange("q c t -> q (c t)").bitcast(F32).rearrange("q (c u) -> q c u", u=2)
                    nc.scalar.copy(out=dst, in_=w[:, i].rearrange("q u c -> q c u"))
            for i in range(2):
                hs = slice(h * HALF, (h + 1) * HALF)
                nc.vector.quantize_mx(out=xq[i][:, hs].bitcast(E4), scales=xs[i][:, hs], in_=il[i][:].rearrange("q c t -> q (c t)"))

        wq, ws = [], []

        def w_load(i, g, h):
            t = sb.tile([P, J, HALF], BF16, name="in16", tag="in16", bufs=16)
            src = (Wk, Wv)[i].rearrange("(g p j) c -> g p j c", p=P, j=J)
            nc.sync.dma_start(out=t[:], in_=src[g][:, :, h * HALF:(h + 1) * HALF])
            return t

        def w_part(i, g, h, raw):
            if len(wq) == i:
                t = sb.tile([P, 2, H], U32, name="in32", tag="in32", bufs=4, align_bytes=64)
                wq.append(t)
                t = const.tile([P, 2, H], U8, name="ws%d" % i, align_bytes=64)
                ws.append(t)
            hs = slice(h * HALF, (h + 1) * HALF)
            il = il_tile()
            nc.vector.tensor_tensor(
                out=il[:], in0=raw[:].rearrange("p j c -> p c j"),
                in1=tm_b[i][:, hs].unsqueeze(2).to_broadcast([P, HALF, 4]), op=ALU.mult,
            )
            nc.vector.quantize_mx(out=wq[i][:, g, hs].bitcast(E4), scales=ws[i][:, g, hs], in_=il[:].rearrange("p c t -> p (c t)"))

        for h in range(2):
            nc.vector.tensor_scalar(out=inp["bb", h][:], in0=inp["bb", h][:], scalar1=-1.0, scalar2=None, op0=ALU.mult)

        tstage = {0: stage_t(0)}
        x_half(0)
        tstage[1] = stage_t(1)
        x_half(1)
        w_jobs = []
        parts, quant = {}, {}
        for b in range(N_CH + 2):
            if b + 2 < N_CH:
                tstage[b + 2] = stage_t(b + 2)
            if b < N_CH:
                parts[b] = stage_c(b, tstage.pop(b))
            if b == 3:
                for i in range(2):
                    for g in range(2):
                        for h in range(2):
                            w_jobs.append((i, g, h, w_load(i, g, h)))
            if 1 <= b <= N_CH:
                quant[b - 1] = stage_s(b - 1, parts.pop(b - 1))
            if b >= 2:
                stage_w(b - 2, *quant.pop(b - 2))
            if b in (4, 8):
                stage_b(b // 4 - 1)
            if b >= 4:
                for job in w_jobs[2 * (b - 4):2 * (b - 4) + 2]:
                    w_part(*job)

        out_rows = out_0.rearrange("(p j) c -> j p c", j=J)
        pools = [ps_tc, ps_mm]
        n_grp = 0
        for j in range(J):
            js = slice(j * P, (j + 1) * P)
            ot = sb.tile([P, H], F32, name="ot", tag="ot", bufs=3)
            for n in range(2):
                ns = slice(n * HALF, (n + 1) * HALF)
                acc = pools[n]([P, HALF], F32)
                order = [(g, i) for g in range(2) for i in (1, 0)]
                for m, (g, i) in enumerate(order):
                    codes, scales = cq[("dk", "dv")[i], g]
                    nc.tensor.matmul_mx(
                        out=acc[:], lhsT=codes[:, js].bitcast(E5), lhsT_scale=scales[:, js],
                        rhs=wq[i][:, g, ns].bitcast(E4), rhs_scale=ws[i][:, g, ns], start=(m == 0), stop=(m == 3),
                    )
                if n == 0:
                    nc.scalar.copy(out=ot[:, ns], in_=acc[:])
                else:
                    nc.vector.tensor_copy(out=ot[:, ns], in_=acc[:])
            nc.sync.dma_start(out=out_rows[j], in_=ot[:])
